import numpy as np
import ml_dtypes


def mxq(x, axis, fmt="e4m3"):
    dtype, down = {"e4m3": (ml_dtypes.float8_e4m3fn, 7), "e5m2": (ml_dtypes.float8_e5m2, 14)}[fmt]
    v = np.moveaxis(np.asarray(x, np.float32).astype(ml_dtypes.bfloat16).astype(np.float64), axis, -1)
    blocks = v.reshape(v.shape[:-1] + (-1, 32))
    amax = np.abs(blocks).max(-1, keepdims=True)
    byte = np.maximum(np.where(amax > 0, np.frexp(amax)[1] - 1 + 127, 0) - down, 1)
    scale = np.exp2(byte - 127.0)
    codes = (blocks / scale).astype(np.float32).astype(dtype).astype(np.float64)
    return np.moveaxis((codes * scale).reshape(v.shape), -1, axis)


BF16 = ml_dtypes.bfloat16


def bf(x):
    return np.asarray(x, np.float32).astype(BF16)


def f64(x):
    return np.asarray(x).astype(np.float64)


B, C, H, W = 4, 1024, 32, 32
M = H * W


def setup_inputs():
    noise = np.random.standard_normal((B, C, H, W))
    shared = np.random.standard_normal((B, 1, H, W))
    gain = np.random.standard_normal((B, C, 1, 1))
    offset = np.random.standard_normal((B, C, 1, 1))
    return {"x": bf(noise + 0.7 * gain * shared + 0.5 * offset)}


def reference(x):
    xf = f64(x).reshape(B, C, M)
    xc = xf - np.mean(xf, axis=2, keepdims=True)
    xq = mxq(xc, 2, "e4m3")
    return (xq @ xq.transpose(0, 2, 1)) / M

@@ -1,0 +1,212 @@
+from contextlib import ExitStack
+
+import concourse.mybir as mybir
+from concourse.masks import make_identity
+
+FP8X4 = mybir.dt.float8_e4m3fn_x4
+BF16 = mybir.dt.bfloat16
+F32 = mybir.dt.float32
+U32 = mybir.dt.uint32
+U8 = mybir.dt.uint8
+ALU = mybir.AluOpType
+FUNC = mybir.ActivationFunctionType
+AXIS = mybir.AxisListType
+
+P = 128
+IMAGES = 4
+CHANNELS = 1024
+POSITIONS = 1024
+FLOPS = 2 * IMAGES * CHANNELS * CHANNELS * POSITIONS
+
+HALF = POSITIONS // 2
+TILE_CH = P // 2
+CHUNK_TILES = 4
+CHUNK_CH = CHUNK_TILES * TILE_CH
+CHUNKS = CHANNELS // CHUNK_CH
+ALL_CHUNKS = IMAGES * CHUNKS
+N_TILE = 512
+M_TILES = CHANNELS // P
+N_TILES = CHANNELS // N_TILE
+
+
+def tile_covpool_t_kernel(tc, x, out):
+    nc = tc.nc
+    xv = x.rearrange("b c h w -> b (c h w)").rearrange("b (t p f) -> b p t f", p=P, f=HALF)
+    with ExitStack() as ctx:
+        const = ctx.enter_context(tc.tile_pool(name="const", bufs=1))
+        xin = ctx.enter_context(tc.tile_pool(name="xin", bufs=ALL_CHUNKS))
+        small = ctx.enter_context(tc.tile_pool(name="small", bufs=4))
+        work = ctx.enter_context(tc.tile_pool(name="work", bufs=3))
+        quant = ctx.enter_context(tc.tile_pool(name="quant", bufs=2))
+        outs = ctx.enter_context(tc.tile_pool(name="outs", bufs=OUT_BUFS))
+        ps_t = ctx.enter_context(tc.psum_pool(name="ps_t", bufs=3))
+        ps_m = ctx.enter_context(tc.psum_pool(name="ps_m", bufs=1))
+        ps_a = ctx.enter_context(tc.psum_pool(name="ps_a", bufs=4))
+        ctx.enter_context(tc.manual_schedule())
+
+        xq, sums, mean_ps, xc, pt, gr, codes, scales, acc, res = {}, {}, {}, {}, {}, {}, {}, {}, {}, {}
+
+        def load(q):
+            b, c = divmod(q, CHUNKS)
+            xq[q] = xin.tile([P, CHUNK_TILES, HALF], BF16, name="xq")
+            nc.sync.dma_start(out=xq[q][:], in_=xv[b, :, c * CHUNK_TILES : (c + 1) * CHUNK_TILES, :])
+
+        for q in range(ALL_CHUNKS):
+            load(q)
+
+        ident = const.tile([P, P], BF16, name="ident")
+        make_identity(nc, ident[:])
+        pair = const.tile([P, TILE_CH], F32, name="pair")
+        nc.vector.tensor_reduce(out=pair[:], in_=ident[:].rearrange("p (c j) -> p c j", j=2), axis=AXIS.X, op=ALU.add)
+        spread = const.tile([P, TILE_CH, 2], F32, name="spread")
+        nc.vector.tensor_scalar(
+            out=spread[:], in0=pair[:].unsqueeze(2).to_broadcast([P, TILE_CH, 2]), scalar1=1.0 / POSITIONS, scalar2=None, op0=ALU.mult
+        )
+        junk = const.tile([P, HALF], BF16, name="junk")
+
+        junk_a = const.tile([P, HALF], BF16, name="junk_a")
+
+        def row_sums(q):
+            nv = V_SUMS(q)
+            sums[q] = small.tile([P, CHUNK_TILES], F32, name="sums")
+            if nv < CHUNK_TILES:
+                sums_a[q] = small.tile([P, CHUNK_TILES], F32, name="sums_a")
+            for t in range(CHUNK_TILES):
+                if t < nv:
+                    nc.vector.tensor_scalar(
+                        out=junk[:], in0=xq[q][:, t, :], scalar1=1.0, scalar2=None, op0=ALU.mult, op1=ALU.add,
+                        accum_out=sums[q][:, t : t + 1],
+                    )
+                else:
+                    nc.scalar.activation(out=junk_a[:], in_=xq[q][:, t, :], func=FUNC.Copy, accum_out=sums_a[q][:, t - nv : t - nv + 1])
+
+        def means(q):
+            nv = V_SUMS(q)
+            mean_ps[q] = ps_m.tile([P, CHUNK_TILES], F32, name="mean_ps")
+            lhsT = spread[:].rearrange("p c j -> p (c j)")
+            nc.tensor.matmul(out=mean_ps[q][:, 0:nv], lhsT=lhsT, rhs=sums[q][:, 0:nv], start=True, stop=True)
+            if nv < CHUNK_TILES:
+                nc.tensor.matmul(out=mean_ps[q][:, nv:], lhsT=lhsT, rhs=sums_a[q][:, 0 : CHUNK_TILES - nv], start=True, stop=True)
+
+        def centre(q):
+            mean = small.tile([P, CHUNK_TILES], F32, name="mean")
+            nc.vector.tensor_copy(out=mean[:], in_=mean_ps[q][:])
+            xc[q] = work.tile([P, CHUNK_TILES, HALF], BF16, name="xc")
+            for t in range(CHUNK_TILES):
+                nc.vector.tensor_scalar(
+                    out=xc[q][:, t, :], in0=xq[q][:, t, :], scalar1=mean[:, t : t + 1], scalar2=None, op0=ALU.subtract
+                )
+
+        def transposes(q):
+            for g in range(2):
+                pt[q, g] = ps_t.tile([P, 2, CHUNK_CH, 2], BF16, name="pt")
+                for u in range(2):
+                    for t in range(CHUNK_TILES):
+                        blk = 2 * g + u
+                        nc.tensor.transpose(
+                            out=pt[q, g][:, u, t * TILE_CH : (t + 1) * TILE_CH, :].rearrange("p m j -> p (m j)"),
+                            in_=xc[q][:, t, blk * P : (blk + 1) * P],
+                            identity=ident[:],
+                        )
+
+        def regroup(q):
+            gr[q] = work.tile([P, 2, 4 * CHUNK_CH], BF16, name="gr", align_bytes=64)
+            for g in range(2):
+                dst = gr[q][:, g, :].rearrange("p (m u j) -> p m u j", u=2, j=2)
+                src = pt[q, g][:].rearrange("p u m j -> p m u j")
+                if V_REGROUP(q, g):
+                    nc.vector.tensor_copy(out=dst, in_=src)
+                else:
+                    nc.scalar.copy(out=dst, in_=src)
+
+        def quantise(q):
+            b, c = divmod(q, CHUNKS)
+            if c == 0:
+                codes[b] = quant.tile([P, 2, CHANNELS], U32, name="codes", align_bytes=64)
+                scales[b] = quant.tile([P, 2, CHANNELS], U8, name="scales", align_bytes=64)
+            cols = slice(c * CHUNK_CH, (c + 1) * CHUNK_CH)
+            for g in range(2):
+                nc.vector.quantize_mx(out=codes[b][:, g, cols].bitcast(FP8X4), scales=scales[b][:, g, cols], in_=gr[q][:, g, :])
+
+        def product(b, m, n):
+            rows = slice(m * P, (m + 1) * P)
+            cols = slice(n * N_TILE, (n + 1) * N_TILE)
+            acc[b, m, n] = ps_a.tile([P, N_TILE], F32, name="acc")
+            for g in range(2):
+                nc.tensor.matmul_mx(
+                    out=acc[b, m, n][:],
+                    lhsT=codes[b][:, g, rows].bitcast(FP8X4),
+                    lhsT_scale=scales[b][:, g, rows],
+                    rhs=codes[b][:, g, cols].bitcast(FP8X4),
+                    rhs_scale=scales[b][:, g, cols],
+                    start=(g == 0),
+                    stop=(g == 1),
+                )
+
+        def leave(b, m, n):
+            rows = slice(m * P, (m + 1) * P)
+            cols = slice(n * N_TILE, (n + 1) * N_TILE)
+            res = outs.tile([P, N_TILE], F32, name="res")
+            if V_LEAVE(b, m, n):
+                nc.vector.tensor_scalar(out=res[:], in0=acc[b, m, n][:], scalar1=1.0 / POSITIONS, scalar2=None, op0=ALU.mult)
+            else:
+                nc.scalar.activation(out=res[:], in_=acc[b, m, n][:], func=FUNC.Copy, scale=1.0 / POSITIONS)
+            nc.sync.dma_start(out=out[b, rows, cols], in_=res[:])
+
+        def products(lst):
+            for k in range(0, len(lst), 2):
+                for it in lst[k : k + 2]:
+                    product(*it)
+                for it in lst[k : k + 2]:
+                    leave(*it)
+
+        sums_a, left = {}, {}
+        work_of = PLAN()
+        row_sums(0)
+        row_sums(1)
+        means(0)
+        centre(0)
+        for i in range(len(work_of)):
+            if i + 2 < ALL_CHUNKS:
+                row_sums(i + 2)
+            if i + 1 < ALL_CHUNKS:
+                means(i + 1)
+            if i < ALL_CHUNKS:
+                transposes(i)
+                regroup(i)
+            if i + 1 < ALL_CHUNKS:
+                centre(i + 1)
+            if i < ALL_CHUNKS:
+                quantise(i)
+            products(work_of[i])
+
+
+def V_SUMS(q):
+    return 2 if q < 6 else 4
+
+
+def V_REGROUP(q, g):
+    return g == 1 and q >= 4
+
+
+def V_LEAVE(b, m, n):
+    return b == 3 and n == 1
+
+
+def PLAN():
+    groups = []
+    for b in range(IMAGES):
+        for n in range(N_TILES):
+            for m in range(M_TILES):
+                groups.append((CHUNKS * b + max(m // 2, 2 * n + 1), b, n, m))
+    groups = sorted(groups)
+    plan = []
+    while groups:
+        i = len(plan)
+        take = [g for g in groups if g[0] + 1 <= i][: 4]
+        plan.append([(g[1], g[3], g[2]) for g in take])
+        groups = [g for g in groups if g not in take]
+    return plan
+
+
+OUT_BUFS = 24

@@ -20,10 +20,8 @@ FLOPS = 2 * IMAGES * CHANNELS * CHANNELS * POSITIONS
 
 HALF = POSITIONS // 2
 TILE_CH = P // 2
-CHUNK_TILES = 4
-CHUNK_CH = CHUNK_TILES * TILE_CH
-CHUNKS = CHANNELS // CHUNK_CH
-ALL_CHUNKS = IMAGES * CHUNKS
+TILES = CHANNELS // TILE_CH
+BANK_TILES = 4
 N_TILE = 512
 M_TILES = CHANNELS // P
 N_TILES = CHANNELS // N_TILE
@@ -32,27 +30,26 @@ N_TILES = CHANNELS // N_TILE
 def tile_covpool_t_kernel(tc, x, out):
     nc = tc.nc
     xv = x.rearrange("b c h w -> b (c h w)").rearrange("b (t p f) -> b p t f", p=P, f=HALF)
+    chunks = CHUNK_LIST()
+    nq = len(chunks)
     with ExitStack() as ctx:
         const = ctx.enter_context(tc.tile_pool(name="const", bufs=1))
-        xin = ctx.enter_context(tc.tile_pool(name="xin", bufs=ALL_CHUNKS))
+        xin = ctx.enter_context(tc.tile_pool(name="xin", bufs=1))
         small = ctx.enter_context(tc.tile_pool(name="small", bufs=4))
         work = ctx.enter_context(tc.tile_pool(name="work", bufs=3))
         quant = ctx.enter_context(tc.tile_pool(name="quant", bufs=2))
         outs = ctx.enter_context(tc.tile_pool(name="outs", bufs=OUT_BUFS))
-        ps_t = ctx.enter_context(tc.psum_pool(name="ps_t", bufs=3))
-        ps_m = ctx.enter_context(tc.psum_pool(name="ps_m", bufs=1))
-        ps_a = ctx.enter_context(tc.psum_pool(name="ps_a", bufs=4))
+        ps_t = ctx.enter_context(tc.psum_pool(name="ps_t", bufs=PT_BUFS))
+        ps_a = ctx.enter_context(tc.psum_pool(name="ps_a", bufs=8 - PT_BUFS))
         ctx.enter_context(tc.manual_schedule())
 
-        xq, sums, mean_ps, xc, pt, gr, codes, scales, acc, res = {}, {}, {}, {}, {}, {}, {}, {}, {}, {}
+        xq, sums, mean, xc, pt, gr, codes, scales, acc = {}, {}, {}, {}, {}, {}, {}, {}, {}
 
-        def load(q):
-            b, c = divmod(q, CHUNKS)
-            xq[q] = xin.tile([P, CHUNK_TILES, HALF], BF16, name="xq")
-            nc.sync.dma_start(out=xq[q][:], in_=xv[b, :, c * CHUNK_TILES : (c + 1) * CHUNK_TILES, :])
-
-        for q in range(ALL_CHUNKS):
-            load(q)
+        for q in range(nq):
+            b, t0, nt = chunks[q]
+            xq[q] = xin.tile([P, nt, HALF], BF16, name="xq%d" % q)
+            for s in range(0, nt, LOAD_TILES(q)):
+                nc.sync.dma_start(out=xq[q][:, s : s + LOAD_TILES(q), :], in_=xv[b, :, t0 + s : t0 + s + LOAD_TILES(q), :])
 
         ident = const.tile([P, P], BF16, name="ident")
         make_identity(nc, ident[:])
@@ -63,68 +60,71 @@ def tile_covpool_t_kernel(tc, x, out):
             out=spread[:], in0=pair[:].unsqueeze(2).to_broadcast([P, TILE_CH, 2]), scalar1=1.0 / POSITIONS, scalar2=None, op0=ALU.mult
         )
         junk = const.tile([P, HALF], BF16, name="junk")
-
         junk_a = const.tile([P, HALF], BF16, name="junk_a")
 
         def row_sums(q):
-            nv = V_SUMS(q)
-            sums[q] = small.tile([P, CHUNK_TILES], F32, name="sums")
-            if nv < CHUNK_TILES:
-                sums_a[q] = small.tile([P, CHUNK_TILES], F32, name="sums_a")
-            for t in range(CHUNK_TILES):
+            nt = chunks[q][2]
+            nv = V_SUMS(q, nt)
+            sums[q] = small.tile([P, 2, 8], F32, name="sums")
+            for t in range(nt):
                 if t < nv:
                     nc.vector.tensor_scalar(
                         out=junk[:], in0=xq[q][:, t, :], scalar1=1.0, scalar2=None, op0=ALU.mult, op1=ALU.add,
-                        accum_out=sums[q][:, t : t + 1],
+                        accum_out=sums[q][:, 0, t : t + 1],
                     )
                 else:
-                    nc.scalar.activation(out=junk_a[:], in_=xq[q][:, t, :], func=FUNC.Copy, accum_out=sums_a[q][:, t - nv : t - nv + 1])
+                    nc.scalar.activation(out=junk_a[:], in_=xq[q][:, t, :], func=FUNC.Copy, accum_out=sums[q][:, 1, t - nv : t - nv + 1])
 
         def means(q):
-            nv = V_SUMS(q)
-            mean_ps[q] = ps_m.tile([P, CHUNK_TILES], F32, name="mean_ps")
-            lhsT = spread[:].rearrange("p c j -> p (c j)")
-            nc.tensor.matmul(out=mean_ps[q][:, 0:nv], lhsT=lhsT, rhs=sums[q][:, 0:nv], start=True, stop=True)
-            if nv < CHUNK_TILES:
-                nc.tensor.matmul(out=mean_ps[q][:, nv:], lhsT=lhsT, rhs=sums_a[q][:, 0 : CHUNK_TILES - nv], start=True, stop=True)
+            nt = chunks[q][2]
+            nv = V_SUMS(q, nt)
+            mean_ps = ps_a.tile([P, 8], F32, name="mean_ps", tag="acc")
+            rhs = sums[q][:, 0, 0:nt] if nv == nt else sums[q][:, :, 0:nv]
+            nc.tensor.matmul(out=mean_ps[:, 0:nt], lhsT=spread[:].rearrange("p c j -> p (c j)"), rhs=rhs, start=True, stop=True)
+            mean[q] = small.tile([P, 8], F32, name="mean")
+            nc.scalar.copy(out=mean[q][:, 0:nt], in_=mean_ps[:, 0:nt])
 
         def centre(q):
-            mean = small.tile([P, CHUNK_TILES], F32, name="mean")
-            nc.vector.tensor_copy(out=mean[:], in_=mean_ps[q][:])
-            xc[q] = work.tile([P, CHUNK_TILES, HALF], BF16, name="xc")
-            for t in range(CHUNK_TILES):
+            nt = chunks[q][2]
+            xc[q] = work.tile([P, nt, HALF], BF16, name="xc")
+            for t in range(nt):
                 nc.vector.tensor_scalar(
-                    out=xc[q][:, t, :], in0=xq[q][:, t, :], scalar1=mean[:, t : t + 1], scalar2=None, op0=ALU.subtract
+                    out=xc[q][:, t, :], in0=xq[q][:, t, :], scalar1=mean[q][:, t : t + 1], scalar2=None, op0=ALU.subtract
                 )
 
         def transposes(q):
-            for g in range(2):
-                pt[q, g] = ps_t.tile([P, 2, CHUNK_CH, 2], BF16, name="pt")
-                for u in range(2):
-                    for t in range(CHUNK_TILES):
-                        blk = 2 * g + u
-                        nc.tensor.transpose(
-                            out=pt[q, g][:, u, t * TILE_CH : (t + 1) * TILE_CH, :].rearrange("p m j -> p (m j)"),
-                            in_=xc[q][:, t, blk * P : (blk + 1) * P],
-                            identity=ident[:],
-                        )
+            nt = chunks[q][2]
+            for h in range(nt // BANK_TILES):
+                for g in range(2):
+                    pt[q, h, g] = ps_t.tile([P, 2, BANK_TILES * TILE_CH, 2], BF16, name="pt")
+                    for u in range(2):
+                        for t in range(BANK_TILES):
+                            blk = 2 * g + u
+                            nc.tensor.transpose(
+                                out=pt[q, h, g][:, u, t * TILE_CH : (t + 1) * TILE_CH, :].rearrange("p m j -> p (m j)"),
+                                in_=xc[q][:, h * BANK_TILES + t, blk * P : (blk + 1) * P],
+                                identity=ident[:],
+                            )
 
         def regroup(q):
-            gr[q] = work.tile([P, 2, 4 * CHUNK_CH], BF16, name="gr", align_bytes=64)
-            for g in range(2):
-                dst = gr[q][:, g, :].rearrange("p (m u j) -> p m u j", u=2, j=2)
-                src = pt[q, g][:].rearrange("p u m j -> p m u j")
-                if V_REGROUP(q, g):
-                    nc.vector.tensor_copy(out=dst, in_=src)
-                else:
-                    nc.scalar.copy(out=dst, in_=src)
+            nt = chunks[q][2]
+            gr[q] = work.tile([P, 2, 4 * nt * TILE_CH], BF16, name="gr", align_bytes=64)
+            w = 4 * BANK_TILES * TILE_CH
+            for h in range(nt // BANK_TILES):
+                for g in range(2):
+                    dst = gr[q][:, g, h * w : (h + 1) * w].rearrange("p (m u j) -> p m u j", u=2, j=2)
+                    src = pt[q, h, g][:].rearrange("p u m j -> p m u j")
+                    if V_REGROUP(q, h, g):
+                        nc.vector.tensor_copy(out=dst, in_=src)
+                    else:
+                        nc.scalar.copy(out=dst, in_=src)
 
         def quantise(q):
-            b, c = divmod(q, CHUNKS)
-            if c == 0:
+            b, t0, nt = chunks[q]
+            if t0 == 0:
                 codes[b] = quant.tile([P, 2, CHANNELS], U32, name="codes", align_bytes=64)
                 scales[b] = quant.tile([P, 2, CHANNELS], U8, name="scales", align_bytes=64)
-            cols = slice(c * CHUNK_CH, (c + 1) * CHUNK_CH)
+            cols = slice(t0 * TILE_CH, (t0 + nt) * TILE_CH)
             for g in range(2):
                 nc.vector.quantize_mx(out=codes[b][:, g, cols].bitcast(FP8X4), scales=scales[b][:, g, cols], in_=gr[q][:, g, :])
 
@@ -160,32 +160,79 @@ def tile_covpool_t_kernel(tc, x, out):
                 for it in lst[k : k + 2]:
                     leave(*it)
 
-        sums_a, left = {}, {}
-        work_of = PLAN()
-        row_sums(0)
-        row_sums(1)
-        means(0)
-        centre(0)
+        work_of = PLAN(chunks)
+        for stage in PROLOGUE:
+            if stage == "a":
+                row_sums(0)
+            if stage == "b":
+                means(0)
+            if stage == "c":
+                row_sums(1)
+            if stage == "d":
+                centre(0)
         for i in range(len(work_of)):
-            if i + 2 < ALL_CHUNKS:
-                row_sums(i + 2)
-            if i + 1 < ALL_CHUNKS:
-                means(i + 1)
-            if i < ALL_CHUNKS:
-                transposes(i)
-                regroup(i)
-            if i + 1 < ALL_CHUNKS:
-                centre(i + 1)
-            if i < ALL_CHUNKS:
-                quantise(i)
-            products(work_of[i])
+            for stage in ORDER:
+                if stage == "M" and i + 1 < nq:
+                    means(i + 1)
+                if stage == "S" and i + 2 < nq:
+                    row_sums(i + 2)
+                if stage == "T" and i < nq:
+                    transposes(i)
+                if stage == "R" and i < nq:
+                    regroup(i)
+                if stage == "C" and i + 1 < nq:
+                    centre(i + 1)
+                if stage == "Q" and i < nq:
+                    quantise(i)
+                if stage == "P":
+                    products(work_of[i])
 
 
-def V_SUMS(q):
-    return 2 if q < 6 else 4
+def PLAN(chunks):
+    ready = {}
+    for q in range(len(chunks)):
+        b, t0, nt = chunks[q]
+        for t in range(t0, t0 + nt):
+            ready[b, t] = q
+    groups = []
+    for b in range(IMAGES):
+        for n in range(N_TILES):
+            for m in range(M_TILES):
+                groups.append((max(ready[b, 2 * m + 1], ready[b, 8 * n + 7]), b, n, m))
+    groups = sorted(groups)
+    plan = []
+    while groups:
+        i = len(plan)
+        cap = CAP(chunks[i][2]) if i < len(chunks) else 99
+        take = [g for g in groups if g[0] + LAG <= i][:cap]
+        plan.append([(g[1], g[3], g[2]) for g in take])
+        groups = [g for g in groups if g not in take]
+    return plan
 
 
-def V_REGROUP(q, g):
+def CHUNK_LIST():
+    lst = []
+    for b in range(IMAGES):
+        t0 = 0
+        for nt in [[4,4,4,4],[8,8],[8,8],[8,8]][b]:
+            lst.append((b, t0, nt))
+            t0 += nt
+    return lst
+
+
+def LOAD_TILES(q):
+    return 4
+
+
+def CAP(nt):
+    return nt
+
+
+def V_SUMS(q, nt):
+    return nt // 2 if q < 5 else nt
+
+
+def V_REGROUP(q, h, g):
     return g == 1 and q >= 4
 
 
@@ -193,20 +240,8 @@ def V_LEAVE(b, m, n):
     return b == 3 and n == 1
 
 
-def PLAN():
-    groups = []
-    for b in range(IMAGES):
-        for n in range(N_TILES):
-            for m in range(M_TILES):
-                groups.append((CHUNKS * b + max(m // 2, 2 * n + 1), b, n, m))
-    groups = sorted(groups)
-    plan = []
-    while groups:
-        i = len(plan)
-        take = [g for g in groups if g[0] + 1 <= i][: 4]
-        plan.append([(g[1], g[3], g[2]) for g in take])
-        groups = [g for g in groups if g not in take]
-    return plan
-
-
+LAG = 1
 OUT_BUFS = 24
+PT_BUFS = 4
+ORDER = "SMTRCQP"
+PROLOGUE = "acbd"

@@ -233,7 +233,7 @@ def V_SUMS(q, nt):
 
 
 def V_REGROUP(q, h, g):
-    return g == 1 and q >= 4
+    return False
 
 
 def V_LEAVE(b, m, n):

@@ -10,7 +10,6 @@ U32 = mybir.dt.uint32
 U8 = mybir.dt.uint8
 ALU = mybir.AluOpType
 FUNC = mybir.ActivationFunctionType
-AXIS = mybir.AxisListType
 
 P = 128
 IMAGES = 4
@@ -43,7 +42,7 @@ def tile_covpool_t_kernel(tc, x, out):
         ps_a = ctx.enter_context(tc.psum_pool(name="ps_a", bufs=8 - PT_BUFS))
         ctx.enter_context(tc.manual_schedule())
 
-        xq, sums, mean, xc, pt, gr, codes, scales, acc = {}, {}, {}, {}, {}, {}, {}, {}, {}
+        xq, turned, both, mean, xc, pt, gr, codes, scales, acc = {}, {}, {}, {}, {}, {}, {}, {}, {}, {}
 
         for q in range(nq):
             b, t0, nt = chunks[q]
@@ -53,43 +52,59 @@ def tile_covpool_t_kernel(tc, x, out):
 
         ident = const.tile([P, P], BF16, name="ident")
         make_identity(nc, ident[:])
-        pair = const.tile([P, TILE_CH], F32, name="pair")
-        nc.vector.tensor_reduce(out=pair[:], in_=ident[:].rearrange("p (c j) -> p c j", j=2), axis=AXIS.X, op=ALU.add)
-        spread = const.tile([P, TILE_CH, 2], F32, name="spread")
-        nc.vector.tensor_scalar(
-            out=spread[:], in0=pair[:].unsqueeze(2).to_broadcast([P, TILE_CH, 2]), scalar1=1.0 / POSITIONS, scalar2=None, op0=ALU.mult
-        )
         junk = const.tile([P, HALF], BF16, name="junk")
         junk_a = const.tile([P, HALF], BF16, name="junk_a")
 
-        def row_sums(q):
-            nt = chunks[q][2]
-            nv = V_SUMS(q, nt)
-            sums[q] = small.tile([P, 2, 8], F32, name="sums")
-            for t in range(nt):
-                if t < nv:
-                    nc.vector.tensor_scalar(
-                        out=junk[:], in0=xq[q][:, t, :], scalar1=1.0, scalar2=None, op0=ALU.mult, op1=ALU.add,
-                        accum_out=sums[q][:, 0, t : t + 1],
-                    )
-                else:
-                    nc.scalar.activation(out=junk_a[:], in_=xq[q][:, t, :], func=FUNC.Copy, accum_out=sums[q][:, 1, t - nv : t - nv + 1])
+        sum_tiles = [const.tile([P, 32], F32, name="sums%d" % k, align_bytes=64) for k in range(SUM_TILES)]
+        for k in range(SUM_TILES):
+            nc.vector.memset(sum_tiles[k][:], 0.0)
 
-        def means(q):
-            nt = chunks[q][2]
-            nv = V_SUMS(q, nt)
-            mean_ps = ps_a.tile([P, 8], F32, name="mean_ps", tag="acc")
-            rhs = sums[q][:, 0, 0:nt] if nv == nt else sums[q][:, :, 0:nv]
-            nc.tensor.matmul(out=mean_ps[:, 0:nt], lhsT=spread[:].rearrange("p c j -> p (c j)"), rhs=rhs, start=True, stop=True)
-            mean[q] = small.tile([P, 8], F32, name="mean")
-            nc.scalar.copy(out=mean[q][:, 0:nt], in_=mean_ps[:, 0:nt])
+        def column(q, t):
+            nv = V_SUMS(q, chunks[q][2])
+            return t if t < nv else 8 + t - nv
+
+        def row_sum(q, t):
+            dst = sum_tiles[q % SUM_TILES][:, column(q, t) : column(q, t) + 1]
+            if column(q, t) < 8:
+                nc.vector.tensor_scalar(
+                    out=junk[:], in0=xq[q][:, t, :], scalar1=1.0 / POSITIONS, scalar2=None, op0=ALU.mult, op1=ALU.add, accum_out=dst
+                )
+            else:
+                nc.scalar.activation(out=junk_a[:], in_=xq[q][:, t, :], func=FUNC.Copy, scale=1.0 / POSITIONS, accum_out=dst)
+
+        def mean_step(q, k):
+            if k == 0:
+                turned[q] = small.tile([P, 32], F32, name="turned", align_bytes=64)
+                nc.vector.transpose(out=turned[q][:], in_=sum_tiles[q % SUM_TILES][:])
+            if k == 1:
+                both[q] = small.tile([P, 32], F32, name="both", align_bytes=64)
+                halves = turned[q][:].rearrange("p (c j) -> p c j", j=2)
+                nc.vector.tensor_tensor(
+                    out=both[q][:].rearrange("p (c j) -> p c j", j=2),
+                    in0=halves[:, :, 0:1].to_broadcast([P, 16, 2]),
+                    in1=halves[:, :, 1:2].to_broadcast([P, 16, 2]),
+                    op=ALU.add,
+                )
+            if k == 2:
+                mean[q] = small.tile([P, 32], F32, name="mean", align_bytes=64)
+                nc.vector.transpose(out=mean[q][:], in_=both[q][:])
+
+        def sums_and_means(qs, qm):
+            todo_s = [(qs, t) for t in range(chunks[qs][2])] if qs < nq else []
+            todo_m = [(qm, k) for k in range(3)] if qm < nq else []
+            for k in range(max(len(todo_s), len(todo_m))):
+                if k < len(todo_m):
+                    mean_step(*todo_m[k])
+                if k < len(todo_s):
+                    row_sum(*todo_s[k])
 
         def centre(q):
             nt = chunks[q][2]
             xc[q] = work.tile([P, nt, HALF], BF16, name="xc")
             for t in range(nt):
                 nc.vector.tensor_scalar(
-                    out=xc[q][:, t, :], in0=xq[q][:, t, :], scalar1=mean[q][:, t : t + 1], scalar2=None, op0=ALU.subtract
+                    out=xc[q][:, t, :], in0=xq[q][:, t, :], scalar1=mean[q][:, column(q, t) : column(q, t) + 1], scalar2=None,
+                    op0=ALU.subtract,
                 )
 
         def transposes(q):
@@ -161,31 +176,19 @@ def tile_covpool_t_kernel(tc, x, out):
                     leave(*it)
 
         work_of = PLAN(chunks)
-        for stage in PROLOGUE:
-            if stage == "a":
-                row_sums(0)
-            if stage == "b":
-                means(0)
-            if stage == "c":
-                row_sums(1)
-            if stage == "d":
-                centre(0)
+        sums_and_means(0, nq)
+        sums_and_means(1, 0)
+        centre(0)
         for i in range(len(work_of)):
-            for stage in ORDER:
-                if stage == "M" and i + 1 < nq:
-                    means(i + 1)
-                if stage == "S" and i + 2 < nq:
-                    row_sums(i + 2)
-                if stage == "T" and i < nq:
-                    transposes(i)
-                if stage == "R" and i < nq:
-                    regroup(i)
-                if stage == "C" and i + 1 < nq:
-                    centre(i + 1)
-                if stage == "Q" and i < nq:
-                    quantise(i)
-                if stage == "P":
-                    products(work_of[i])
+            sums_and_means(i + 2, i + 1)
+            if i < nq:
+                transposes(i)
+                regroup(i)
+            if i + 1 < nq:
+                centre(i + 1)
+            if i < nq:
+                quantise(i)
+            products(work_of[i])
 
 
 def PLAN(chunks):
@@ -214,7 +217,7 @@ def CHUNK_LIST():
     lst = []
     for b in range(IMAGES):
         t0 = 0
-        for nt in [[4,4,4,4],[8,8],[8,8],[8,8]][b]:
+        for nt in [[4,4,4,4],[4,4,4,4],[4,4,4,4],[4,4,4,4]][b]:
             lst.append((b, t0, nt))
             t0 += nt
     return lst
@@ -233,7 +236,7 @@ def V_SUMS(q, nt):
 
 
 def V_REGROUP(q, h, g):
-    return False
+    return g == 1 and q >= 4 and q % 2 == 1
 
 
 def V_LEAVE(b, m, n):
@@ -242,6 +245,5 @@ def V_LEAVE(b, m, n):
 
 LAG = 1
 OUT_BUFS = 24
-PT_BUFS = 4
-ORDER = "SMTRCQP"
-PROLOGUE = "acbd"
+PT_BUFS = 3
+SUM_TILES = 4

@@ -17,129 +17,93 @@ CHANNELS = 1024
 POSITIONS = 1024
 FLOPS = 2 * IMAGES * CHANNELS * CHANNELS * POSITIONS
 
-HALF = POSITIONS // 2
-TILE_CH = P // 2
-TILES = CHANNELS // TILE_CH
-BANK_TILES = 4
+ROWS = 2
+CHUNK = P * ROWS
+CHUNKS = CHANNELS // CHUNK
+NQ = IMAGES * CHUNKS
 N_TILE = 512
 M_TILES = CHANNELS // P
 N_TILES = CHANNELS // N_TILE
 
+PT_BUFS = 4
+LAG = 1
+CAP = 4
+
 
 def tile_covpool_t_kernel(tc, x, out):
     nc = tc.nc
-    xv = x.rearrange("b c h w -> b (c h w)").rearrange("b (t p f) -> b p t f", p=P, f=HALF)
-    chunks = CHUNK_LIST()
-    nq = len(chunks)
+    xv = x.rearrange("b c h w -> b (c h w)").rearrange("b (q p f) -> b q p f", q=CHUNKS, p=P)
     with ExitStack() as ctx:
         const = ctx.enter_context(tc.tile_pool(name="const", bufs=1))
         xin = ctx.enter_context(tc.tile_pool(name="xin", bufs=1))
         small = ctx.enter_context(tc.tile_pool(name="small", bufs=4))
         work = ctx.enter_context(tc.tile_pool(name="work", bufs=3))
         quant = ctx.enter_context(tc.tile_pool(name="quant", bufs=2))
-        outs = ctx.enter_context(tc.tile_pool(name="outs", bufs=OUT_BUFS))
+        outs = ctx.enter_context(tc.tile_pool(name="outs", bufs=16))
         ps_t = ctx.enter_context(tc.psum_pool(name="ps_t", bufs=PT_BUFS))
         ps_a = ctx.enter_context(tc.psum_pool(name="ps_a", bufs=8 - PT_BUFS))
         ctx.enter_context(tc.manual_schedule())
 
-        xq, turned, both, mean, xc, pt, gr, codes, scales, acc = {}, {}, {}, {}, {}, {}, {}, {}, {}, {}
+        xq, mean, xc, pt, gr, codes, scales, acc, res = {}, {}, {}, {}, {}, {}, {}, {}, {}
 
-        for q in range(nq):
-            b, t0, nt = chunks[q]
-            xq[q] = xin.tile([P, nt, HALF], BF16, name="xq%d" % q)
-            for s in range(0, nt, LOAD_TILES(q)):
-                nc.sync.dma_start(out=xq[q][:, s : s + LOAD_TILES(q), :], in_=xv[b, :, t0 + s : t0 + s + LOAD_TILES(q), :])
+        for q in range(NQ):
+            xq[q] = xin.tile([P, ROWS, POSITIONS], BF16, name="xq%d" % q)
+            nc.sync.dma_start(out=xq[q][:].rearrange("p j f -> p (j f)"), in_=xv[q // CHUNKS, q % CHUNKS])
 
-        ident = const.tile([P, P], BF16, name="ident")
+        ident = const.tile([P, P], F32, name="ident")
         make_identity(nc, ident[:])
-        junk = const.tile([P, HALF], BF16, name="junk")
-        junk_a = const.tile([P, HALF], BF16, name="junk_a")
+        junk_v = const.tile([P, POSITIONS], BF16, name="junk_v")
+        junk_s = const.tile([P, POSITIONS], BF16, name="junk_s")
 
-        sum_tiles = [const.tile([P, 32], F32, name="sums%d" % k, align_bytes=64) for k in range(SUM_TILES)]
-        for k in range(SUM_TILES):
-            nc.vector.memset(sum_tiles[k][:], 0.0)
-
-        def column(q, t):
-            nv = V_SUMS(q, chunks[q][2])
-            return t if t < nv else 8 + t - nv
-
-        def row_sum(q, t):
-            dst = sum_tiles[q % SUM_TILES][:, column(q, t) : column(q, t) + 1]
-            if column(q, t) < 8:
-                nc.vector.tensor_scalar(
-                    out=junk[:], in0=xq[q][:, t, :], scalar1=1.0 / POSITIONS, scalar2=None, op0=ALU.mult, op1=ALU.add, accum_out=dst
-                )
+        def row_sum(q, j):
+            if j == 0:
+                mean[q] = small.tile([P, ROWS], F32, name="mean")
+            dst = mean[q][:, j : j + 1]
+            if j == 1 and S_SUM(q):
+                nc.scalar.activation(out=junk_s[:], in_=xq[q][:, j, :], func=FUNC.Copy, scale=1.0 / POSITIONS, accum_out=dst)
             else:
-                nc.scalar.activation(out=junk_a[:], in_=xq[q][:, t, :], func=FUNC.Copy, scale=1.0 / POSITIONS, accum_out=dst)
-
-        def mean_step(q, k):
-            if k == 0:
-                turned[q] = small.tile([P, 32], F32, name="turned", align_bytes=64)
-                nc.vector.transpose(out=turned[q][:], in_=sum_tiles[q % SUM_TILES][:])
-            if k == 1:
-                both[q] = small.tile([P, 32], F32, name="both", align_bytes=64)
-                halves = turned[q][:].rearrange("p (c j) -> p c j", j=2)
-                nc.vector.tensor_tensor(
-                    out=both[q][:].rearrange("p (c j) -> p c j", j=2),
-                    in0=halves[:, :, 0:1].to_broadcast([P, 16, 2]),
-                    in1=halves[:, :, 1:2].to_broadcast([P, 16, 2]),
-                    op=ALU.add,
-                )
-            if k == 2:
-                mean[q] = small.tile([P, 32], F32, name="mean", align_bytes=64)
-                nc.vector.transpose(out=mean[q][:], in_=both[q][:])
-
-        def sums_and_means(qs, qm):
-            todo_s = [(qs, t) for t in range(chunks[qs][2])] if qs < nq else []
-            todo_m = [(qm, k) for k in range(3)] if qm < nq else []
-            for k in range(max(len(todo_s), len(todo_m))):
-                if k < len(todo_m):
-                    mean_step(*todo_m[k])
-                if k < len(todo_s):
-                    row_sum(*todo_s[k])
-
-        def centre(q):
-            nt = chunks[q][2]
-            xc[q] = work.tile([P, nt, HALF], BF16, name="xc")
-            for t in range(nt):
                 nc.vector.tensor_scalar(
-                    out=xc[q][:, t, :], in0=xq[q][:, t, :], scalar1=mean[q][:, column(q, t) : column(q, t) + 1], scalar2=None,
-                    op0=ALU.subtract,
+                    out=junk_v[:], in0=xq[q][:, j, :], scalar1=1.0 / POSITIONS, scalar2=None, op0=ALU.mult, op1=ALU.add, accum_out=dst
                 )
+
+        def centre(q, j):
+            if j == 0:
+                xc[q] = work.tile([P, ROWS, POSITIONS], BF16, name="xc")
+            nc.vector.tensor_scalar(
+                out=xc[q][:, j, :], in0=xq[q][:, j, :], scalar1=mean[q][:, j : j + 1], scalar2=None, op0=ALU.subtract
+            )
+
+        def sums_and_centres(qs, qc):
+            for j in range(ROWS):
+                if qs < NQ:
+                    row_sum(qs, j)
+                if qc < NQ:
+                    centre(qc, j)
 
         def transposes(q):
-            nt = chunks[q][2]
-            for h in range(nt // BANK_TILES):
-                for g in range(2):
-                    pt[q, h, g] = ps_t.tile([P, 2, BANK_TILES * TILE_CH, 2], BF16, name="pt")
-                    for u in range(2):
-                        for t in range(BANK_TILES):
-                            blk = 2 * g + u
-                            nc.tensor.transpose(
-                                out=pt[q, h, g][:, u, t * TILE_CH : (t + 1) * TILE_CH, :].rearrange("p m j -> p (m j)"),
-                                in_=xc[q][:, h * BANK_TILES + t, blk * P : (blk + 1) * P],
-                                identity=ident[:],
-                            )
+            for g in range(2):
+                pt[q, g] = ps_t.tile([P, 2, ROWS, P], F32, name="pt")
+                for u in range(2):
+                    for j in range(ROWS):
+                        blk = 2 * g + u
+                        nc.tensor.transpose(
+                            out=pt[q, g][:, u, j, :],
+                            in_=xc[q][:, j, :].bitcast(F32)[:, blk * P : (blk + 1) * P],
+                            identity=ident[:],
+                        )
 
         def regroup(q):
-            nt = chunks[q][2]
-            gr[q] = work.tile([P, 2, 4 * nt * TILE_CH], BF16, name="gr", align_bytes=64)
-            w = 4 * BANK_TILES * TILE_CH
-            for h in range(nt // BANK_TILES):
-                for g in range(2):
-                    dst = gr[q][:, g, h * w : (h + 1) * w].rearrange("p (m u j) -> p m u j", u=2, j=2)
-                    src = pt[q, h, g][:].rearrange("p u m j -> p m u j")
-                    if V_REGROUP(q, h, g):
-                        nc.vector.tensor_copy(out=dst, in_=src)
-                    else:
-                        nc.scalar.copy(out=dst, in_=src)
+            gr[q] = work.tile([P, 2, 4 * CHUNK], BF16, name="gr", align_bytes=64)
+            for g in range(2):
+                dst = gr[q][:, g, :].bitcast(F32).rearrange("p (m j u) -> p m j u", j=ROWS, u=2)
+                nc.scalar.copy(out=dst, in_=pt[q, g][:].rearrange("p u j m -> p m j u"))
 
         def quantise(q):
-            b, t0, nt = chunks[q]
-            if t0 == 0:
+            b, c = divmod(q, CHUNKS)
+            if c == 0:
                 codes[b] = quant.tile([P, 2, CHANNELS], U32, name="codes", align_bytes=64)
                 scales[b] = quant.tile([P, 2, CHANNELS], U8, name="scales", align_bytes=64)
-            cols = slice(t0 * TILE_CH, (t0 + nt) * TILE_CH)
+            cols = slice(c * CHUNK, (c + 1) * CHUNK)
             for g in range(2):
                 nc.vector.quantize_mx(out=codes[b][:, g, cols].bitcast(FP8X4), scales=scales[b][:, g, cols], in_=gr[q][:, g, :])
 
@@ -158,92 +122,48 @@ def tile_covpool_t_kernel(tc, x, out):
                     stop=(g == 1),
                 )
 
-        def leave(b, m, n):
+        def leave(b, m, n, on_vector):
             rows = slice(m * P, (m + 1) * P)
             cols = slice(n * N_TILE, (n + 1) * N_TILE)
-            res = outs.tile([P, N_TILE], F32, name="res")
-            if V_LEAVE(b, m, n):
-                nc.vector.tensor_scalar(out=res[:], in0=acc[b, m, n][:], scalar1=1.0 / POSITIONS, scalar2=None, op0=ALU.mult)
+            if n == 0:
+                res[b, m] = outs.tile([P, CHANNELS], F32, name="res")
+            dst = res[b, m][:, cols]
+            if on_vector:
+                nc.vector.tensor_scalar(out=dst, in0=acc[b, m, n][:], scalar1=1.0 / POSITIONS, scalar2=None, op0=ALU.mult)
             else:
-                nc.scalar.activation(out=res[:], in_=acc[b, m, n][:], func=FUNC.Copy, scale=1.0 / POSITIONS)
-            nc.sync.dma_start(out=out[b, rows, cols], in_=res[:])
+                nc.scalar.activation(out=dst, in_=acc[b, m, n][:], func=FUNC.Copy, scale=1.0 / POSITIONS)
+            if n == N_TILES - 1:
+                nc.sync.dma_start(out=out[b, rows, :], in_=res[b, m][:])
 
-        def products(lst):
-            for k in range(0, len(lst), 2):
-                for it in lst[k : k + 2]:
-                    product(*it)
-                for it in lst[k : k + 2]:
-                    leave(*it)
-
-        work_of = PLAN(chunks)
-        sums_and_means(0, nq)
-        sums_and_means(1, 0)
-        centre(0)
-        for i in range(len(work_of)):
-            sums_and_means(i + 2, i + 1)
-            if i < nq:
+        plan = PLAN()
+        sums_and_centres(0, NQ)
+        sums_and_centres(1, 0)
+        for i in range(len(plan)):
+            sums_and_centres(i + 2, i + 1)
+            if i < NQ:
                 transposes(i)
                 regroup(i)
-            if i + 1 < nq:
-                centre(i + 1)
-            if i < nq:
                 quantise(i)
-            products(work_of[i])
+            for k in range(len(plan[i])):
+                product(*plan[i][k])
+                leave(*plan[i][k], k % 2 == 1 if i >= NQ else k == 3)
 
 
-def PLAN(chunks):
-    ready = {}
-    for q in range(len(chunks)):
-        b, t0, nt = chunks[q]
-        for t in range(t0, t0 + nt):
-            ready[b, t] = q
+def PLAN():
     groups = []
     for b in range(IMAGES):
-        for n in range(N_TILES):
-            for m in range(M_TILES):
-                groups.append((max(ready[b, 2 * m + 1], ready[b, 8 * n + 7]), b, n, m))
-    groups = sorted(groups)
+        for m in range(M_TILES):
+            for n in range(N_TILES):
+                early = n == 0 and m < M_TILES // 2
+                groups.append((CHUNKS * b + (1 if early else CHUNKS - 1), b, m, n))
+    todo = sorted(groups)
     plan = []
-    while groups:
-        i = len(plan)
-        cap = CAP(chunks[i][2]) if i < len(chunks) else 99
-        take = [g for g in groups if g[0] + LAG <= i][:cap]
-        plan.append([(g[1], g[3], g[2]) for g in take])
-        groups = [g for g in groups if g not in take]
+    while todo:
+        take = [t for t in todo if t[0] + LAG <= len(plan)][:CAP]
+        todo = [t for t in todo if t not in take]
+        plan.append([t[1:] for t in take])
     return plan
 
 
-def CHUNK_LIST():
-    lst = []
-    for b in range(IMAGES):
-        t0 = 0
-        for nt in [[4,4,4,4],[4,4,4,4],[4,4,4,4],[4,4,4,4]][b]:
-            lst.append((b, t0, nt))
-            t0 += nt
-    return lst
-
-
-def LOAD_TILES(q):
-    return 4
-
-
-def CAP(nt):
-    return nt
-
-
-def V_SUMS(q, nt):
-    return nt // 2 if q < 5 else nt
-
-
-def V_REGROUP(q, h, g):
-    return g == 1 and q >= 4 and q % 2 == 1
-
-
-def V_LEAVE(b, m, n):
-    return b == 3 and n == 1
-
-
-LAG = 1
-OUT_BUFS = 24
-PT_BUFS = 3
-SUM_TILES = 4
+def S_SUM(q):
+    return q < 5

@@ -73,18 +73,12 @@ def tile_covpool_t_kernel(tc, x, out):
                 out=xc[q][:, j, :], in0=xq[q][:, j, :], scalar1=mean[q][:, j : j + 1], scalar2=None, op0=ALU.subtract
             )
 
-        def sums_and_centres(qs, qc):
-            for j in range(ROWS):
-                if qs < NQ:
-                    row_sum(qs, j)
-                if qc < NQ:
-                    centre(qc, j)
-
         def transposes(q):
             for g in range(2):
                 pt[q, g] = ps_t.tile([P, 2, ROWS, P], F32, name="pt")
-                for u in range(2):
-                    for j in range(ROWS):
+            for j in range(ROWS):
+                for g in range(2):
+                    for u in range(2):
                         blk = 2 * g + u
                         nc.tensor.transpose(
                             out=pt[q, g][:, u, j, :],
@@ -98,14 +92,13 @@ def tile_covpool_t_kernel(tc, x, out):
                 dst = gr[q][:, g, :].bitcast(F32).rearrange("p (m j u) -> p m j u", j=ROWS, u=2)
                 nc.scalar.copy(out=dst, in_=pt[q, g][:].rearrange("p u j m -> p m j u"))
 
-        def quantise(q):
+        def quantise(q, g):
             b, c = divmod(q, CHUNKS)
-            if c == 0:
+            if c == 0 and g == 0:
                 codes[b] = quant.tile([P, 2, CHANNELS], U32, name="codes", align_bytes=64)
                 scales[b] = quant.tile([P, 2, CHANNELS], U8, name="scales", align_bytes=64)
             cols = slice(c * CHUNK, (c + 1) * CHUNK)
-            for g in range(2):
-                nc.vector.quantize_mx(out=codes[b][:, g, cols].bitcast(FP8X4), scales=scales[b][:, g, cols], in_=gr[q][:, g, :])
+            nc.vector.quantize_mx(out=codes[b][:, g, cols].bitcast(FP8X4), scales=scales[b][:, g, cols], in_=gr[q][:, g, :])
 
         def product(b, m, n):
             rows = slice(m * P, (m + 1) * P)
@@ -122,45 +115,77 @@ def tile_covpool_t_kernel(tc, x, out):
                     stop=(g == 1),
                 )
 
+        def mirror(b, m):
+            acc[b, m, 0] = ps_a.tile([P, N_TILE], F32, name="acc")
+            cols = slice(m * P, (m + 1) * P)
+            for k in range(N_TILE // P):
+                nc.tensor.transpose(out=acc[b, m, 0][:, k * P : (k + 1) * P], in_=res[b, k][:, cols], identity=ident[:])
+
         def leave(b, m, n, on_vector):
             rows = slice(m * P, (m + 1) * P)
             cols = slice(n * N_TILE, (n + 1) * N_TILE)
-            if n == 0:
+            if (b, m) not in res:
                 res[b, m] = outs.tile([P, CHANNELS], F32, name="res")
             dst = res[b, m][:, cols]
-            if on_vector:
+            if MIRRORED(m, n):
+                if on_vector:
+                    nc.vector.tensor_copy(out=dst, in_=acc[b, m, n][:])
+                else:
+                    nc.scalar.copy(out=dst, in_=acc[b, m, n][:])
+            elif on_vector:
                 nc.vector.tensor_scalar(out=dst, in0=acc[b, m, n][:], scalar1=1.0 / POSITIONS, scalar2=None, op0=ALU.mult)
             else:
                 nc.scalar.activation(out=dst, in_=acc[b, m, n][:], func=FUNC.Copy, scale=1.0 / POSITIONS)
-            if n == N_TILES - 1:
+            left.append((b, m))
+            if (b, m) == (IMAGES - 1, M_TILES - 1):
+                nc.sync.dma_start(out=out[b, rows, cols], in_=dst)
+            elif len([t for t in left if t == (b, m)]) == N_TILES:
                 nc.sync.dma_start(out=out[b, rows, :], in_=res[b, m][:])
 
+        left = []
         plan = PLAN()
-        sums_and_centres(0, NQ)
-        sums_and_centres(1, 0)
+        row_sum(0, 0)
+        row_sum(0, 1)
+        centre(0, 0)
+        centre(0, 1)
+        row_sum(1, 0)
+        row_sum(1, 1)
         for i in range(len(plan)):
-            sums_and_centres(i + 2, i + 1)
+            if i + 1 < NQ:
+                centre(i + 1, 0)
+                centre(i + 1, 1)
             if i < NQ:
                 transposes(i)
                 regroup(i)
-                quantise(i)
+            for g in range(2):
+                if i < NQ:
+                    quantise(i, g)
+                if i + 2 < NQ:
+                    row_sum(i + 2, g)
             for k in range(len(plan[i])):
-                product(*plan[i][k])
-                leave(*plan[i][k], k % 2 == 1 if i >= NQ else k == 3)
+                b, m, n = plan[i][k]
+                if MIRRORED(m, n):
+                    mirror(b, m)
+                else:
+                    product(b, m, n)
+                leave(b, m, n, k % 2 == 1 if i >= NQ or i < 6 else k == 3)
+
+
+def MIRRORED(m, n):
+    return n == 0 and m >= M_TILES // 2
 
 
 def PLAN():
+    half = M_TILES // 2
     groups = []
     for b in range(IMAGES):
-        for m in range(M_TILES):
-            for n in range(N_TILES):
-                early = n == 0 and m < M_TILES // 2
-                groups.append((CHUNKS * b + (1 if early else CHUNKS - 1), b, m, n))
-    todo = sorted(groups)
+        groups += [(CHUNKS * b + 1, b, m, 0) for m in range(half)]
+        groups += [(CHUNKS * b + 3, b, m, 1) for m in range(M_TILES)]
+        groups += [(CHUNKS * b + 3, b, m, 0) for m in range(half, M_TILES)]
     plan = []
-    while todo:
-        take = [t for t in todo if t[0] + LAG <= len(plan)][:CAP]
-        todo = [t for t in todo if t not in take]
+    while groups:
+        take = [t for t in groups if t[0] + LAG <= len(plan)][:CAP]
+        groups = [t for t in groups if t not in take]
         plan.append([t[1:] for t in take])
     return plan
 

@@ -21,12 +21,11 @@ ROWS = 2
 CHUNK = P * ROWS
 CHUNKS = CHANNELS // CHUNK
 NQ = IMAGES * CHUNKS
-N_TILE = 512
-M_TILES = CHANNELS // P
-N_TILES = CHANNELS // N_TILE
 
 PT_BUFS = 4
 LAG = 1
+M_LAG = 2
+M_CAP = 1
 CAP = 4
 
 
@@ -39,7 +38,7 @@ def tile_covpool_t_kernel(tc, x, out):
         small = ctx.enter_context(tc.tile_pool(name="small", bufs=4))
         work = ctx.enter_context(tc.tile_pool(name="work", bufs=3))
         quant = ctx.enter_context(tc.tile_pool(name="quant", bufs=2))
-        outs = ctx.enter_context(tc.tile_pool(name="outs", bufs=16))
+        outs = ctx.enter_context(tc.tile_pool(name="outs", bufs=8))
         ps_t = ctx.enter_context(tc.psum_pool(name="ps_t", bufs=PT_BUFS))
         ps_a = ctx.enter_context(tc.psum_pool(name="ps_a", bufs=8 - PT_BUFS))
         ctx.enter_context(tc.manual_schedule())
@@ -100,49 +99,52 @@ def tile_covpool_t_kernel(tc, x, out):
             cols = slice(c * CHUNK, (c + 1) * CHUNK)
             nc.vector.quantize_mx(out=codes[b][:, g, cols].bitcast(FP8X4), scales=scales[b][:, g, cols], in_=gr[q][:, g, :])
 
-        def product(b, m, n):
-            rows = slice(m * P, (m + 1) * P)
-            cols = slice(n * N_TILE, (n + 1) * N_TILE)
-            acc[b, m, n] = ps_a.tile([P, N_TILE], F32, name="acc")
-            for g in range(2):
-                nc.tensor.matmul_mx(
-                    out=acc[b, m, n][:],
-                    lhsT=codes[b][:, g, rows].bitcast(FP8X4),
-                    lhsT_scale=scales[b][:, g, rows],
-                    rhs=codes[b][:, g, cols].bitcast(FP8X4),
-                    rhs_scale=scales[b][:, g, cols],
-                    start=(g == 0),
-                    stop=(g == 1),
-                )
+        def product(b, r, c):
+            acc[b, r, c] = ps_a.tile([P, 2, CHUNK], F32, name="acc")
+            if r > c:
+                for z in range(2):
+                    rows = slice((2 * r + z) * P, (2 * r + z + 1) * P)
+                    for k in range(2):
+                        nc.tensor.transpose(out=acc[b, r, c][:, z, k * P : (k + 1) * P], in_=res[b, c][:, k, rows], identity=ident[:])
+                return
+            cols = slice(c * CHUNK, (c + 1) * CHUNK)
+            for z in range(2):
+                rows = slice((2 * r + z) * P, (2 * r + z + 1) * P)
+                for g in range(2):
+                    nc.tensor.matmul_mx(
+                        out=acc[b, r, c][:, z, :],
+                        lhsT=codes[b][:, g, rows].bitcast(FP8X4),
+                        lhsT_scale=scales[b][:, g, rows],
+                        rhs=codes[b][:, g, cols].bitcast(FP8X4),
+                        rhs_scale=scales[b][:, g, cols],
+                        start=(g == 0),
+                        stop=(g == 1),
+                    )
 
-        def mirror(b, m):
-            acc[b, m, 0] = ps_a.tile([P, N_TILE], F32, name="acc")
-            cols = slice(m * P, (m + 1) * P)
-            for k in range(N_TILE // P):
-                nc.tensor.transpose(out=acc[b, m, 0][:, k * P : (k + 1) * P], in_=res[b, k][:, cols], identity=ident[:])
-
-        def leave(b, m, n, on_vector):
-            rows = slice(m * P, (m + 1) * P)
-            cols = slice(n * N_TILE, (n + 1) * N_TILE)
-            if (b, m) not in res:
-                res[b, m] = outs.tile([P, CHANNELS], F32, name="res")
-            dst = res[b, m][:, cols]
-            if MIRRORED(m, n):
+        def leave(b, r, c, on_vector):
+            if (b, r) not in res:
+                res[b, r] = outs.tile([P, 2, CHANNELS], F32, name="res")
+            dst = res[b, r][:, :, c * CHUNK : (c + 1) * CHUNK]
+            src = acc[b, r, c][:]
+            if r > c:
                 if on_vector:
-                    nc.vector.tensor_copy(out=dst, in_=acc[b, m, n][:])
+                    nc.vector.tensor_copy(out=dst, in_=src)
                 else:
-                    nc.scalar.copy(out=dst, in_=acc[b, m, n][:])
+                    nc.scalar.copy(out=dst, in_=src)
             elif on_vector:
-                nc.vector.tensor_scalar(out=dst, in0=acc[b, m, n][:], scalar1=1.0 / POSITIONS, scalar2=None, op0=ALU.mult)
+                nc.vector.tensor_scalar(out=dst, in0=src, scalar1=1.0 / POSITIONS, scalar2=None, op0=ALU.mult)
             else:
-                nc.scalar.activation(out=dst, in_=acc[b, m, n][:], func=FUNC.Copy, scale=1.0 / POSITIONS)
-            left.append((b, m))
-            if (b, m) == (IMAGES - 1, M_TILES - 1):
-                nc.sync.dma_start(out=out[b, rows, cols], in_=dst)
-            elif len([t for t in left if t == (b, m)]) == N_TILES:
-                nc.sync.dma_start(out=out[b, rows, :], in_=res[b, m][:])
+                nc.scalar.activation(out=dst, in_=src, func=FUNC.Copy, scale=1.0 / POSITIONS)
+            left.add((b, r, c))
+            width = CHUNKS // 2 if b == IMAGES - 1 else CHUNKS
+            first = c // width * width
+            if all((b, r, k) in left for k in range(first, first + width)):
+                cols = slice(first * CHUNK, (first + width) * CHUNK)
+                for z in range(2):
+                    rows = slice((2 * r + z) * P, (2 * r + z + 1) * P)
+                    nc.sync.dma_start(out=out[b, rows, cols], in_=res[b, r][:, z, cols])
 
-        left = []
+        left = set()
         plan = PLAN()
         row_sum(0, 0)
         row_sum(0, 1)
@@ -163,32 +165,27 @@ def tile_covpool_t_kernel(tc, x, out):
                 if i + 2 < NQ:
                     row_sum(i + 2, g)
             for k in range(len(plan[i])):
-                b, m, n = plan[i][k]
-                if MIRRORED(m, n):
-                    mirror(b, m)
-                else:
-                    product(b, m, n)
-                leave(b, m, n, k % 2 == 1 if i >= NQ or i < 6 else k == 3)
-
-
-def MIRRORED(m, n):
-    return n == 0 and m >= M_TILES // 2
+                product(*plan[i][k])
+                leave(*plan[i][k], k % 2 == 1 if i >= NQ or i < 4 else k == 3)
 
 
 def PLAN():
-    half = M_TILES // 2
-    groups = []
-    for b in range(IMAGES):
-        groups += [(CHUNKS * b + 1, b, m, 0) for m in range(half)]
-        groups += [(CHUNKS * b + 3, b, m, 1) for m in range(M_TILES)]
-        groups += [(CHUNKS * b + 3, b, m, 0) for m in range(half, M_TILES)]
-    plan = []
-    while groups:
-        take = [t for t in groups if t[0] + LAG <= len(plan)][:CAP]
-        groups = [t for t in groups if t not in take]
-        plan.append([t[1:] for t in take])
+    direct = [(CHUNKS * b + c, b, r, c) for b in range(IMAGES) for c in range(CHUNKS) for r in range(c + 1)]
+    mirrored = [(b, r, c) for b in range(IMAGES) for r in range(CHUNKS) for c in range(r)]
+    when, plan = {}, []
+    while direct or mirrored:
+        i = len(plan)
+        m_now = [t for t in mirrored if when.get((t[0], t[2], t[1]), i) + M_LAG <= i]
+        d_now = [t for t in direct if t[0] + LAG <= i]
+        nm = min(len(m_now), CAP, max(M_CAP, CAP - len(d_now)))
+        m_now, d_now = m_now[:nm], d_now[: CAP - nm]
+        mirrored = [t for t in mirrored if t not in m_now]
+        direct = [t for t in direct if t not in d_now]
+        plan.append(m_now + [t[1:] for t in d_now])
+        for t in plan[i]:
+            when[t] = i
     return plan
 
 
 def S_SUM(q):
-    return q < 5
+    return q < 3

@@ -136,7 +136,7 @@ def tile_covpool_t_kernel(tc, x, out):
             else:
                 nc.scalar.activation(out=dst, in_=src, func=FUNC.Copy, scale=1.0 / POSITIONS)
             left.add((b, r, c))
-            width = CHUNKS // 2 if b == IMAGES - 1 else CHUNKS
+            width = CHUNKS // 2 if b > 0 else CHUNKS
             first = c // width * width
             if all((b, r, k) in left for k in range(first, first + width)):
                 cols = slice(first * CHUNK, (first + width) * CHUNK)

@@ -136,7 +136,7 @@ def tile_covpool_t_kernel(tc, x, out):
             else:
                 nc.scalar.activation(out=dst, in_=src, func=FUNC.Copy, scale=1.0 / POSITIONS)
             left.add((b, r, c))
-            width = CHUNKS // 2 if b > 0 else CHUNKS
+            width = CHUNKS if b == 0 or (b == IMAGES - 1 and r >= CHUNKS // 2) else CHUNKS // 2
             first = c // width * width
             if all((b, r, k) in left for k in range(first, first + width)):
                 cols = slice(first * CHUNK, (first + width) * CHUNK)
@@ -159,11 +159,13 @@ def tile_covpool_t_kernel(tc, x, out):
             if i < NQ:
                 transposes(i)
                 regroup(i)
-            for g in range(2):
-                if i < NQ:
-                    quantise(i, g)
-                if i + 2 < NQ:
-                    row_sum(i + 2, g)
+            if i + 2 < NQ:
+                row_sum(i + 2, 0)
+            if i < NQ:
+                quantise(i, 0)
+                quantise(i, 1)
+            if i + 2 < NQ:
+                row_sum(i + 2, 1)
             for k in range(len(plan[i])):
                 product(*plan[i][k])
                 leave(*plan[i][k], k % 2 == 1 if i >= NQ or i < 4 else k == 3)

@@ -136,7 +136,10 @@ def tile_covpool_t_kernel(tc, x, out):
             else:
                 nc.scalar.activation(out=dst, in_=src, func=FUNC.Copy, scale=1.0 / POSITIONS)
             left.add((b, r, c))
-            width = CHUNKS if b == 0 or (b == IMAGES - 1 and r >= CHUNKS // 2) else CHUNKS // 2
+            if b == IMAGES - 1:
+                width = (1, 2, CHUNKS, CHUNKS)[r]
+            else:
+                width = CHUNKS if b == 0 else CHUNKS // 2
             first = c // width * width
             if all((b, r, k) in left for k in range(first, first + width)):
                 cols = slice(first * CHUNK, (first + width) * CHUNK)
@@ -168,7 +171,7 @@ def tile_covpool_t_kernel(tc, x, out):
                 row_sum(i + 2, 1)
             for k in range(len(plan[i])):
                 product(*plan[i][k])
-                leave(*plan[i][k], k % 2 == 1 if i >= NQ or i < 4 else k == 3)
+                leave(*plan[i][k], k % 2 == 1 if i >= NQ else k == 3)
 
 
 def PLAN():

@@ -10,6 +10,7 @@ U32 = mybir.dt.uint32
 U8 = mybir.dt.uint8
 ALU = mybir.AluOpType
 FUNC = mybir.ActivationFunctionType
+AXIS = mybir.AxisListType
 
 P = 128
 IMAGES = 4
@@ -27,6 +28,8 @@ LAG = 1
 M_LAG = 2
 M_CAP = 1
 CAP = 4
+SUM_COLS = 64
+T_SUM = 3
 
 
 def tile_covpool_t_kernel(tc, x, out):
@@ -44,13 +47,18 @@ def tile_covpool_t_kernel(tc, x, out):
         ctx.enter_context(tc.manual_schedule())
 
         xq, mean, xc, pt, gr, codes, scales, acc, res = {}, {}, {}, {}, {}, {}, {}, {}, {}
+        sums = {}
 
         for q in range(NQ):
             xq[q] = xin.tile([P, ROWS, POSITIONS], BF16, name="xq%d" % q)
             nc.sync.dma_start(out=xq[q][:].rearrange("p j f -> p (j f)"), in_=xv[q // CHUNKS, q % CHUNKS])
 
+        zeros = const.tile([P, 2 * CHUNK], BF16, name="zeros")
+        nc.vector.memset(zeros[:], 0.0)
         ident = const.tile([P, P], F32, name="ident")
         make_identity(nc, ident[:])
+        ident_mean = const.tile([P, P], BF16, name="ident_mean")
+        nc.vector.tensor_scalar(out=ident_mean[:], in0=ident[:], scalar1=1.0 / POSITIONS, scalar2=None, op0=ALU.mult)
         junk_v = const.tile([P, POSITIONS], BF16, name="junk_v")
         junk_s = const.tile([P, POSITIONS], BF16, name="junk_s")
 
@@ -64,6 +72,29 @@ def tile_covpool_t_kernel(tc, x, out):
                 nc.vector.tensor_scalar(
                     out=junk_v[:], in0=xq[q][:, j, :], scalar1=1.0 / POSITIONS, scalar2=None, op0=ALU.mult, op1=ALU.add, accum_out=dst
                 )
+
+        def warm_up(n):
+            spare = ps_a.tile([P, 2, CHUNK], F32, name="acc")
+            for k in range(n):
+                nc.tensor.matmul(
+                    out=spare[:].rearrange("p z n -> p (z n)"), lhsT=zeros[:, 0:P], rhs=zeros[:], start=True, stop=True
+                )
+
+        def tensor_sums(q):
+            sums[q] = ps_a.tile([P, 2, CHUNK], F32, name="acc")
+            for j in range(ROWS):
+                for k in range(0, POSITIONS, SUM_COLS):
+                    nc.tensor.matmul(
+                        out=sums[q][:, j, 0:SUM_COLS],
+                        lhsT=ident_mean[:],
+                        rhs=xq[q][:, j, k : k + SUM_COLS],
+                        start=(k == 0),
+                        stop=(k + SUM_COLS == POSITIONS),
+                    )
+
+        def fold_sums(q):
+            mean[q] = small.tile([P, ROWS], F32, name="mean")
+            nc.vector.tensor_reduce(out=mean[q][:], in_=sums[q][:, :, 0:SUM_COLS], axis=AXIS.X, op=ALU.add)
 
         def centre(q, j):
             if j == 0:
@@ -139,7 +170,7 @@ def tile_covpool_t_kernel(tc, x, out):
             if b == IMAGES - 1:
                 width = (1, 2, CHUNKS, CHUNKS)[r]
             else:
-                width = CHUNKS if b == 0 else CHUNKS // 2
+                width = CHUNKS if b < 2 else CHUNKS // 2
             first = c // width * width
             if all((b, r, k) in left for k in range(first, first + width)):
                 cols = slice(first * CHUNK, (first + width) * CHUNK)
@@ -149,6 +180,7 @@ def tile_covpool_t_kernel(tc, x, out):
 
         left = set()
         plan = PLAN()
+        warm_up(8)
         row_sum(0, 0)
         row_sum(0, 1)
         centre(0, 0)
@@ -161,13 +193,19 @@ def tile_covpool_t_kernel(tc, x, out):
                 centre(i + 1, 1)
             if i < NQ:
                 transposes(i)
+                if i == 0:
+                    warm_up(2)
+                if i + 2 == T_SUM:
+                    tensor_sums(T_SUM)
                 regroup(i)
-            if i + 2 < NQ:
+            if i + 2 < NQ and i + 2 != T_SUM:
                 row_sum(i + 2, 0)
             if i < NQ:
                 quantise(i, 0)
                 quantise(i, 1)
-            if i + 2 < NQ:
+            if i + 2 == T_SUM:
+                fold_sums(T_SUM)
+            elif i + 2 < NQ:
                 row_sum(i + 2, 1)
             for k in range(len(plan[i])):
                 product(*plan[i][k])
@@ -193,4 +231,4 @@ def PLAN():
 
 
 def S_SUM(q):
-    return q < 3
+    return q < 2

@@ -23,7 +23,7 @@ CHUNK = P * ROWS
 CHUNKS = CHANNELS // CHUNK
 NQ = IMAGES * CHUNKS
 
-PT_BUFS = 4
+PT_BUFS = 3
 LAG = 1
 M_LAG = 2
 M_CAP = 1

@@ -23,13 +23,13 @@ CHUNK = P * ROWS
 CHUNKS = CHANNELS // CHUNK
 NQ = IMAGES * CHUNKS
 
-PT_BUFS = 3
 LAG = 1
 M_LAG = 2
-M_CAP = 1
+M_CAP = 4
 CAP = 4
 SUM_COLS = 64
 T_SUM = 3
+SUMS_FIRST = 4
 
 
 def tile_covpool_t_kernel(tc, x, out):
@@ -42,8 +42,7 @@ def tile_covpool_t_kernel(tc, x, out):
         work = ctx.enter_context(tc.tile_pool(name="work", bufs=3))
         quant = ctx.enter_context(tc.tile_pool(name="quant", bufs=2))
         outs = ctx.enter_context(tc.tile_pool(name="outs", bufs=8))
-        ps_t = ctx.enter_context(tc.psum_pool(name="ps_t", bufs=PT_BUFS))
-        ps_a = ctx.enter_context(tc.psum_pool(name="ps_a", bufs=8 - PT_BUFS))
+        banks = ctx.enter_context(tc.psum_pool(name="banks", bufs=8))
         ctx.enter_context(tc.manual_schedule())
 
         xq, mean, xc, pt, gr, codes, scales, acc, res = {}, {}, {}, {}, {}, {}, {}, {}, {}
@@ -51,7 +50,11 @@ def tile_covpool_t_kernel(tc, x, out):
 
         for q in range(NQ):
             xq[q] = xin.tile([P, ROWS, POSITIONS], BF16, name="xq%d" % q)
-            nc.sync.dma_start(out=xq[q][:].rearrange("p j f -> p (j f)"), in_=xv[q // CHUNKS, q % CHUNKS])
+            if q == 0:
+                for j in range(ROWS):
+                    nc.sync.dma_start(out=xq[q][:, j, :], in_=xv[0, 0][:, j * POSITIONS : (j + 1) * POSITIONS])
+            else:
+                nc.sync.dma_start(out=xq[q][:].rearrange("p j f -> p (j f)"), in_=xv[q // CHUNKS, q % CHUNKS])
 
         zeros = const.tile([P, 2 * CHUNK], BF16, name="zeros")
         nc.vector.memset(zeros[:], 0.0)
@@ -59,7 +62,7 @@ def tile_covpool_t_kernel(tc, x, out):
         make_identity(nc, ident[:])
         ident_mean = const.tile([P, P], BF16, name="ident_mean")
         nc.vector.tensor_scalar(out=ident_mean[:], in0=ident[:], scalar1=1.0 / POSITIONS, scalar2=None, op0=ALU.mult)
-        junk_v = const.tile([P, POSITIONS], BF16, name="junk_v")
+        junk_v = const.tile([P, ROWS, POSITIONS], BF16, name="junk_v")
         junk_s = const.tile([P, POSITIONS], BF16, name="junk_s")
 
         def row_sum(q, j):
@@ -70,18 +73,18 @@ def tile_covpool_t_kernel(tc, x, out):
                 nc.scalar.activation(out=junk_s[:], in_=xq[q][:, j, :], func=FUNC.Copy, scale=1.0 / POSITIONS, accum_out=dst)
             else:
                 nc.vector.tensor_scalar(
-                    out=junk_v[:], in0=xq[q][:, j, :], scalar1=1.0 / POSITIONS, scalar2=None, op0=ALU.mult, op1=ALU.add, accum_out=dst
+                    out=junk_v[:, j, :], in0=xq[q][:, j, :], scalar1=1.0 / POSITIONS, scalar2=None, op0=ALU.mult, op1=ALU.add, accum_out=dst
                 )
 
         def warm_up(n):
-            spare = ps_a.tile([P, 2, CHUNK], F32, name="acc")
+            spare = banks.tile([P, 2, CHUNK], F32, name="bank")
             for k in range(n):
                 nc.tensor.matmul(
                     out=spare[:].rearrange("p z n -> p (z n)"), lhsT=zeros[:, 0:P], rhs=zeros[:], start=True, stop=True
                 )
 
         def tensor_sums(q):
-            sums[q] = ps_a.tile([P, 2, CHUNK], F32, name="acc")
+            sums[q] = banks.tile([P, 2, CHUNK], F32, name="bank")
             for j in range(ROWS):
                 for k in range(0, POSITIONS, SUM_COLS):
                     nc.tensor.matmul(
@@ -105,7 +108,7 @@ def tile_covpool_t_kernel(tc, x, out):
 
         def transposes(q):
             for g in range(2):
-                pt[q, g] = ps_t.tile([P, 2, ROWS, P], F32, name="pt")
+                pt[q, g] = banks.tile([P, 2, ROWS, P], F32, name="bank")
             for j in range(ROWS):
                 for g in range(2):
                     for u in range(2):
@@ -131,7 +134,7 @@ def tile_covpool_t_kernel(tc, x, out):
             nc.vector.quantize_mx(out=codes[b][:, g, cols].bitcast(FP8X4), scales=scales[b][:, g, cols], in_=gr[q][:, g, :])
 
         def product(b, r, c):
-            acc[b, r, c] = ps_a.tile([P, 2, CHUNK], F32, name="acc")
+            acc[b, r, c] = banks.tile([P, 2, CHUNK], F32, name="bank")
             if r > c:
                 for z in range(2):
                     rows = slice((2 * r + z) * P, (2 * r + z + 1) * P)
@@ -200,12 +203,14 @@ def tile_covpool_t_kernel(tc, x, out):
                 regroup(i)
             if i + 2 < NQ and i + 2 != T_SUM:
                 row_sum(i + 2, 0)
+                if i < SUMS_FIRST:
+                    row_sum(i + 2, 1)
+            if i + 2 == T_SUM:
+                fold_sums(T_SUM)
             if i < NQ:
                 quantise(i, 0)
                 quantise(i, 1)
-            if i + 2 == T_SUM:
-                fold_sums(T_SUM)
-            elif i + 2 < NQ:
+            if SUMS_FIRST <= i < NQ - 2 and i + 2 != T_SUM:
                 row_sum(i + 2, 1)
             for k in range(len(plan[i])):
                 product(*plan[i][k])
@@ -231,4 +236,4 @@ def PLAN():
 
 
 def S_SUM(q):
-    return q < 2
+    return q == 1

@@ -25,7 +25,7 @@ NQ = IMAGES * CHUNKS
 
 LAG = 1
 M_LAG = 2
-M_CAP = 4
+M_CAP = 1
 CAP = 4
 SUM_COLS = 64
 T_SUM = 3
@@ -135,7 +135,7 @@ def tile_covpool_t_kernel(tc, x, out):
 
         def product(b, r, c):
             acc[b, r, c] = banks.tile([P, 2, CHUNK], F32, name="bank")
-            if r > c:
+            if MIRROR(r, c):
                 for z in range(2):
                     rows = slice((2 * r + z) * P, (2 * r + z + 1) * P)
                     for k in range(2):
@@ -160,7 +160,7 @@ def tile_covpool_t_kernel(tc, x, out):
                 res[b, r] = outs.tile([P, 2, CHANNELS], F32, name="res")
             dst = res[b, r][:, :, c * CHUNK : (c + 1) * CHUNK]
             src = acc[b, r, c][:]
-            if r > c:
+            if MIRROR(r, c):
                 if on_vector:
                     nc.vector.tensor_copy(out=dst, in_=src)
                 else:
@@ -218,8 +218,15 @@ def tile_covpool_t_kernel(tc, x, out):
 
 
 def PLAN():
-    direct = [(CHUNKS * b + c, b, r, c) for b in range(IMAGES) for c in range(CHUNKS) for r in range(c + 1)]
-    mirrored = [(b, r, c) for b in range(IMAGES) for r in range(CHUNKS) for c in range(r)]
+    direct = [
+        (CHUNKS * b + q, b, r, c)
+        for b in range(IMAGES)
+        for q in range(CHUNKS)
+        for r in range(CHUNKS)
+        for c in range(CHUNKS)
+        if max(r, c) == q and not MIRROR(r, c)
+    ]
+    mirrored = [(b, r, c) for b in range(IMAGES) for r in range(CHUNKS) for c in range(CHUNKS) if MIRROR(r, c)]
     when, plan = {}, []
     while direct or mirrored:
         i = len(plan)
@@ -237,3 +244,7 @@ def PLAN():
 
 def S_SUM(q):
     return q == 1
+
+
+def MIRROR(r, c):
+    return r >= CHUNKS // 2 and c < CHUNKS // 2

@@ -183,7 +183,7 @@ def tile_covpool_t_kernel(tc, x, out):
 
         left = set()
         plan = PLAN()
-        warm_up(8)
+        warm_up(12)
         row_sum(0, 0)
         row_sum(0, 1)
         centre(0, 0)

from contextlib import ExitStack

import concourse.mybir as mybir
from concourse.masks import make_identity

FP8X4 = mybir.dt.float8_e4m3fn_x4
BF16 = mybir.dt.bfloat16
F32 = mybir.dt.float32
U32 = mybir.dt.uint32
U8 = mybir.dt.uint8
ALU = mybir.AluOpType
FUNC = mybir.ActivationFunctionType
AXIS = mybir.AxisListType

P = 128
IMAGES = 4
CHANNELS = 1024
POSITIONS = 1024
FLOPS = 2 * IMAGES * CHANNELS * CHANNELS * POSITIONS

ROWS = 2
CHUNK = P * ROWS
CHUNKS = CHANNELS // CHUNK
NQ = IMAGES * CHUNKS

LAG = 1
M_LAG = 2
M_CAP = 1
CAP = 4
SUM_COLS = 64
T_SUM = 3
SUMS_FIRST = 4


def tile_covpool_t_kernel(tc, x, out):
    nc = tc.nc
    xv = x.rearrange("b c h w -> b (c h w)").rearrange("b (q p f) -> b q p f", q=CHUNKS, p=P)
    with ExitStack() as ctx:
        const = ctx.enter_context(tc.tile_pool(name="const", bufs=1))
        xin = ctx.enter_context(tc.tile_pool(name="xin", bufs=1))
        small = ctx.enter_context(tc.tile_pool(name="small", bufs=4))
        work = ctx.enter_context(tc.tile_pool(name="work", bufs=3))
        quant = ctx.enter_context(tc.tile_pool(name="quant", bufs=2))
        outs = ctx.enter_context(tc.tile_pool(name="outs", bufs=8))
        banks = ctx.enter_context(tc.psum_pool(name="banks", bufs=8))
        ctx.enter_context(tc.manual_schedule())

        xq, mean, xc, pt, gr, codes, scales, acc, res = {}, {}, {}, {}, {}, {}, {}, {}, {}
        sums = {}

        for q in range(NQ):
            xq[q] = xin.tile([P, ROWS, POSITIONS], BF16, name="xq%d" % q)
            if q == 0:
                for j in range(ROWS):
                    nc.sync.dma_start(out=xq[q][:, j, :], in_=xv[0, 0][:, j * POSITIONS : (j + 1) * POSITIONS])
            else:
                nc.sync.dma_start(out=xq[q][:].rearrange("p j f -> p (j f)"), in_=xv[q // CHUNKS, q % CHUNKS])

        zeros = const.tile([P, 2 * CHUNK], BF16, name="zeros")
        nc.vector.memset(zeros[:], 0.0)
        ident = const.tile([P, P], F32, name="ident")
        make_identity(nc, ident[:])
        ident_mean = const.tile([P, P], BF16, name="ident_mean")
        nc.vector.tensor_scalar(out=ident_mean[:], in0=ident[:], scalar1=1.0 / POSITIONS, scalar2=None, op0=ALU.mult)
        junk_v = const.tile([P, ROWS, POSITIONS], BF16, name="junk_v")
        junk_s = const.tile([P, POSITIONS], BF16, name="junk_s")

        def row_sum(q, j):
            if j == 0:
                mean[q] = small.tile([P, ROWS], F32, name="mean")
            dst = mean[q][:, j : j + 1]
            if j == 1 and S_SUM(q):
                nc.scalar.activation(out=junk_s[:], in_=xq[q][:, j, :], func=FUNC.Copy, scale=1.0 / POSITIONS, accum_out=dst)
            else:
                nc.vector.tensor_scalar(
                    out=junk_v[:, j, :], in0=xq[q][:, j, :], scalar1=1.0 / POSITIONS, scalar2=None, op0=ALU.mult, op1=ALU.add, accum_out=dst
                )

        def warm_up(n):
            spare = banks.tile([P, 2, CHUNK], F32, name="bank")
            for k in range(n):
                nc.tensor.matmul(
                    out=spare[:].rearrange("p z n -> p (z n)"), lhsT=zeros[:, 0:P], rhs=zeros[:], start=True, stop=True
                )

        def tensor_sums(q):
            sums[q] = banks.tile([P, 2, CHUNK], F32, name="bank")
            for j in range(ROWS):
                for k in range(0, POSITIONS, SUM_COLS):
                    nc.tensor.matmul(
                        out=sums[q][:, j, 0:SUM_COLS],
                        lhsT=ident_mean[:],
                        rhs=xq[q][:, j, k : k + SUM_COLS],
                        start=(k == 0),
                        stop=(k + SUM_COLS == POSITIONS),
                    )

        def fold_sums(q):
            mean[q] = small.tile([P, ROWS], F32, name="mean")
            nc.vector.tensor_reduce(out=mean[q][:], in_=sums[q][:, :, 0:SUM_COLS], axis=AXIS.X, op=ALU.add)

        def centre(q, j):
            if j == 0:
                xc[q] = work.tile([P, ROWS, POSITIONS], BF16, name="xc")
            nc.vector.tensor_scalar(
                out=xc[q][:, j, :], in0=xq[q][:, j, :], scalar1=mean[q][:, j : j + 1], scalar2=None, op0=ALU.subtract
            )

        def transposes(q):
            for g in range(2):
                pt[q, g] = banks.tile([P, 2, ROWS, P], F32, name="bank")
            for j in range(ROWS):
                for g in range(2):
                    for u in range(2):
                        blk = 2 * g + u
                        nc.tensor.transpose(
                            out=pt[q, g][:, u, j, :],
                            in_=xc[q][:, j, :].bitcast(F32)[:, blk * P : (blk + 1) * P],
                            identity=ident[:],
                        )

        def regroup(q):
            gr[q] = work.tile([P, 2, 4 * CHUNK], BF16, name="gr", align_bytes=64)
            for g in range(2):
                dst = gr[q][:, g, :].bitcast(F32).rearrange("p (m j u) -> p m j u", j=ROWS, u=2)
                nc.scalar.copy(out=dst, in_=pt[q, g][:].rearrange("p u j m -> p m j u"))

        def quantise(q, g):
            b, c = divmod(q, CHUNKS)
            if c == 0 and g == 0:
                codes[b] = quant.tile([P, 2, CHANNELS], U32, name="codes", align_bytes=64)
                scales[b] = quant.tile([P, 2, CHANNELS], U8, name="scales", align_bytes=64)
            cols = slice(c * CHUNK, (c + 1) * CHUNK)
            nc.vector.quantize_mx(out=codes[b][:, g, cols].bitcast(FP8X4), scales=scales[b][:, g, cols], in_=gr[q][:, g, :])

        def product(b, r, c):
            acc[b, r, c] = banks.tile([P, 2, CHUNK], F32, name="bank")
            if MIRROR(r, c):
                for z in range(2):
                    rows = slice((2 * r + z) * P, (2 * r + z + 1) * P)
                    for k in range(2):
                        nc.tensor.transpose(out=acc[b, r, c][:, z, k * P : (k + 1) * P], in_=res[b, c][:, k, rows], identity=ident[:])
                return
            cols = slice(c * CHUNK, (c + 1) * CHUNK)
            for z in range(2):
                rows = slice((2 * r + z) * P, (2 * r + z + 1) * P)
                for g in range(2):
                    nc.tensor.matmul_mx(
                        out=acc[b, r, c][:, z, :],
                        lhsT=codes[b][:, g, rows].bitcast(FP8X4),
                        lhsT_scale=scales[b][:, g, rows],
                        rhs=codes[b][:, g, cols].bitcast(FP8X4),
                        rhs_scale=scales[b][:, g, cols],
                        start=(g == 0),
                        stop=(g == 1),
                    )

        def leave(b, r, c, on_vector):
            if (b, r) not in res:
                res[b, r] = outs.tile([P, 2, CHANNELS], F32, name="res")
            dst = res[b, r][:, :, c * CHUNK : (c + 1) * CHUNK]
            src = acc[b, r, c][:]
            if MIRROR(r, c):
                if on_vector:
                    nc.vector.tensor_copy(out=dst, in_=src)
                else:
                    nc.scalar.copy(out=dst, in_=src)
            elif on_vector:
                nc.vector.tensor_scalar(out=dst, in0=src, scalar1=1.0 / POSITIONS, scalar2=None, op0=ALU.mult)
            else:
                nc.scalar.activation(out=dst, in_=src, func=FUNC.Copy, scale=1.0 / POSITIONS)
            left.add((b, r, c))
            if b == IMAGES - 1:
                width = (1, 2, CHUNKS, CHUNKS)[r]
            else:
                width = CHUNKS if b < 2 else CHUNKS // 2
            first = c // width * width
            if all((b, r, k) in left for k in range(first, first + width)):
                cols = slice(first * CHUNK, (first + width) * CHUNK)
                for z in range(2):
                    rows = slice((2 * r + z) * P, (2 * r + z + 1) * P)
                    nc.sync.dma_start(out=out[b, rows, cols], in_=res[b, r][:, z, cols])

        left = set()
        plan = PLAN()
        warm_up(12)
        row_sum(0, 0)
        row_sum(0, 1)
        centre(0, 0)
        centre(0, 1)
        row_sum(1, 0)
        row_sum(1, 1)
        for i in range(len(plan)):
            if i + 1 < NQ:
                centre(i + 1, 0)
                centre(i + 1, 1)
            if i < NQ:
                transposes(i)
                if i == 0:
                    warm_up(2)
                if i + 2 == T_SUM:
                    tensor_sums(T_SUM)
                regroup(i)
            if i + 2 < NQ and i + 2 != T_SUM:
                row_sum(i + 2, 0)
                if i < SUMS_FIRST:
                    row_sum(i + 2, 1)
            if i + 2 == T_SUM:
                fold_sums(T_SUM)
            if i < NQ:
                quantise(i, 0)
                quantise(i, 1)
            if SUMS_FIRST <= i < NQ - 2 and i + 2 != T_SUM:
                row_sum(i + 2, 1)
            for k in range(len(plan[i])):
                product(*plan[i][k])
                leave(*plan[i][k], k % 2 == 1 if i >= NQ else k == 3)


def PLAN():
    direct = [
        (CHUNKS * b + q, b, r, c)
        for b in range(IMAGES)
        for q in range(CHUNKS)
        for r in range(CHUNKS)
        for c in range(CHUNKS)
        if max(r, c) == q and not MIRROR(r, c)
    ]
    mirrored = [(b, r, c) for b in range(IMAGES) for r in range(CHUNKS) for c in range(CHUNKS) if MIRROR(r, c)]
    when, plan = {}, []
    while direct or mirrored:
        i = len(plan)
        m_now = [t for t in mirrored if when.get((t[0], t[2], t[1]), i) + M_LAG <= i]
        d_now = [t for t in direct if t[0] + LAG <= i]
        nm = min(len(m_now), CAP, max(M_CAP, CAP - len(d_now)))
        m_now, d_now = m_now[:nm], d_now[: CAP - nm]
        mirrored = [t for t in mirrored if t not in m_now]
        direct = [t for t in direct if t not in d_now]
        plan.append(m_now + [t[1:] for t in d_now])
        for t in plan[i]:
            when[t] = i
    return plan


def S_SUM(q):
    return q == 1


def MIRROR(r, c):
    return r >= CHUNKS // 2 and c < CHUNKS // 2
